import numpy as np
import ml_dtypes

BF16 = ml_dtypes.bfloat16


def bf(x):
    return np.asarray(x, np.float32).astype(BF16)


def f32(x):
    return np.asarray(x, np.float32)


def f64(x):
    return np.asarray(x).astype(np.float64)


def striped(idx):
    return np.tile(idx.reshape(-1, 16).T, (8, 1))


B, NN, CI, CO, S, N, K = 16, 128, 512, 512, 4096, 2048, 3
P_EDGE = 0.03


def setup_inputs():
    x = bf(np.random.standard_normal((CI, N)))
    a = f32(np.random.random((NN, NN)) < P_EDGE)
    adj = f32(np.maximum(np.maximum(a, a.T), np.eye(NN, dtype=np.float32)))
    w = bf(np.random.standard_normal((K, CI, CO)) * np.sqrt(2.0 / (CI + CO)))
    bias = f32(0.1 * np.random.standard_normal((CO, 1)))
    base = f32(np.random.standard_normal((CO, S)))
    return {"x": x, "adj": adj, "w": w, "bias": bias, "base": base, "offs": striped(np.random.permutation(S)[:N])}


def reference(x, adj, w, bias, base, offs):
    idx = offs[:16].T.reshape(-1)
    xa, aa, wa = f64(x), f64(adj), f64(w)
    r = 1.0 / np.sqrt(aa.sum(axis=1))
    eye = np.eye(NN)
    lap = eye - r[:, None] * aa * r[None, :]
    t2 = 2.0 * (lap @ lap) - eye
    own = wa[0].T @ xa + f64(bias)
    u1 = (wa[1].T @ xa).reshape(CO, B, NN)
    u2 = (wa[2].T @ xa).reshape(CO, B, NN)
    nb = np.einsum('dim,nm->din', u1, lap) + np.einsum('dim,nm->din', u2, t2)
    out = f64(base).copy()
    out[:, idx] = own + nb.reshape(CO, N)
    return out

@@ -1,0 +1,131 @@
+from contextlib import ExitStack
+
+import concourse.mybir as mybir
+from concourse.masks import make_identity
+
+F32 = mybir.dt.float32
+BF16 = mybir.dt.bfloat16
+U16 = mybir.dt.uint16
+ADD = mybir.AluOpType.add
+MULT = mybir.AluOpType.mult
+SUBTRACT = mybir.AluOpType.subtract
+IDENTITY = mybir.ActivationFunctionType.Identity
+
+P = 128
+ORDERS = 3
+CI = 512
+CO = 512
+N = 2048
+S = 4096
+CB = CI // P
+DB = CO // P
+CHUNK = 512
+NQ = N // CHUNK
+GRAPHS = CHUNK // P
+PAIR = 2
+
+FLOPS = 2 * ORDERS * CI * CO * N + 2 * 2 * P * CO * N + 2 * P * P * P
+
+
+def tile_reschebgc_b_kernel(tc, x, adj, w, bias, base, offs, out):
+    nc = tc.nc
+    with ExitStack() as ctx:
+        held = ctx.enter_context(tc.tile_pool(name="held", bufs=1))
+        mixed = ctx.enter_context(tc.tile_pool(name="mixed", bufs=4))
+        staged = ctx.enter_context(tc.tile_pool(name="staged", bufs=2))
+        psum_setup = ctx.enter_context(tc.psum_pool(name="psum_setup", bufs=1))
+        psum_u = ctx.enter_context(tc.psum_pool(name="psum_u", bufs=3))
+        psum_own = ctx.enter_context(tc.psum_pool(name="psum_own", bufs=2))
+        psum_nb = ctx.enter_context(tc.psum_pool(name="psum_nb", bufs=2))
+
+        adj_sb = held.tile([P, P], F32, name="adj_sb")
+        nc.sync.dma_start(adj_sb[:], adj)
+        w_sb = held.tile([P, ORDERS, CB, CO], BF16, name="w_sb")
+        w_view = w.rearrange("k (cb c) d -> k c cb d", c=P)
+        x_sb = [held.tile([P, CB, CHUNK], BF16, name=f"x_sb{q}") for q in range(NQ)]
+        x_view = x.rearrange("(cb c) j -> c cb j", c=P)
+        nc.sync.dma_start(w_sb[:, 1], w_view[1])
+        nc.sync.dma_start(w_sb[:, 2], w_view[2])
+        nc.sync.dma_start(x_sb[0][:], x_view[:, :, 0:CHUNK])
+        nc.sync.dma_start(w_sb[:, 0], w_view[0])
+        for q in range(1, NQ):
+            nc.sync.dma_start(x_sb[q][:], x_view[:, :, q * CHUNK : (q + 1) * CHUNK])
+        bias_rows = held.tile([DB, P], F32, name="bias_rows")
+        nc.sync.dma_start(bias_rows[:], bias.rearrange("(b d) o -> b (d o)", d=P))
+        offsets = held.tile([P, N // 16], U16, name="offsets")
+        nc.sync.dma_start(offsets[:], offs)
+        windows = [held.tile([P, S], F32, name=f"window{b}") for b in range(DB)]
+        for b in range(DB):
+            nc.sync.dma_start(windows[b][:], base[b * P : (b + 1) * P, :])
+
+        ident = held.tile([P, P], F32, name="ident")
+        make_identity(nc, ident[:])
+        deg = held.tile([P, 1], F32, name="deg")
+        nc.vector.reduce_sum(deg[:], adj_sb[:], axis=mybir.AxisListType.X)
+        root = held.tile([P, 1], F32, name="root")
+        nc.scalar.sqrt(root[:], deg[:])
+        r = held.tile([P, 1], F32, name="r")
+        nc.vector.reciprocal(r[:], root[:])
+        minus_r = held.tile([P, 1], F32, name="minus_r")
+        nc.vector.tensor_scalar_mul(minus_r[:], r[:], -1.0)
+        diag_r = held.tile([P, P], F32, name="diag_r")
+        nc.vector.tensor_scalar_mul(diag_r[:], ident[:], r[:])
+        cols_ps = psum_setup.tile([P, P], F32, name="setup_ps")
+        nc.tensor.matmul(cols_ps[:], lhsT=adj_sb[:], rhs=diag_r[:], start=True, stop=True)
+        lap = held.tile([P, P], BF16, name="lap")
+        nc.vector.scalar_tensor_tensor(lap[:], cols_ps[:], minus_r[:], ident[:], op0=MULT, op1=ADD)
+        square_ps = psum_setup.tile([P, P], F32, name="setup_ps")
+        nc.tensor.matmul(square_ps[:], lhsT=lap[:], rhs=lap[:], start=True, stop=True)
+        cheb2 = held.tile([P, P], BF16, name="cheb2")
+        nc.vector.scalar_tensor_tensor(cheb2[:], square_ps[:], 2.0, ident[:], op0=MULT, op1=SUBTRACT)
+
+        bias_ps = psum_setup.tile([P, P], F32, name="setup_ps")
+        nc.tensor.matmul(
+            bias_ps[:, 0:DB], lhsT=bias_rows[:], rhs=ident[0:DB, 0:DB], start=True, stop=True
+        )
+        bias_col = held.tile([P, DB], F32, name="bias_col")
+        nc.vector.tensor_copy(bias_col[:], bias_ps[:, 0:DB])
+
+        for b in range(DB):
+            d_cols = slice(b * P, (b + 1) * P)
+            own_sb = staged.tile([P, N], F32, name="own_sb")
+            nb_sb = staged.tile([P, N], F32, name="nb_sb")
+            for q in range(NQ):
+                j_cols = slice(q * CHUNK, (q + 1) * CHUNK)
+                u_bf = []
+                for pair in range(GRAPHS // PAIR):
+                    u_ps = psum_u.tile([P, PAIR, 2, P], F32, name="u_ps")
+                    for i in range(PAIR):
+                        g = pair * PAIR + i
+                        for cb in range(CB):
+                            nc.tensor.matmul(
+                                u_ps[:, i],
+                                lhsT=x_sb[q][:, cb, g * P : (g + 1) * P],
+                                rhs=w_sb[:, 1:3, cb, d_cols],
+                                start=(cb == 0),
+                                stop=(cb == CB - 1),
+                            )
+                    u_bf.append(mixed.tile([P, PAIR, 2, P], BF16, name="u_bf"))
+                    nc.scalar.copy(u_bf[pair][:], u_ps[:])
+
+                own_ps = psum_own.tile([P, CHUNK], F32, name="own_ps")
+                for cb in range(CB):
+                    nc.tensor.matmul(
+                        own_ps[:],
+                        lhsT=w_sb[:, 0, cb, d_cols],
+                        rhs=x_sb[q][:, cb, :],
+                        start=(cb == 0),
+                        stop=(cb == CB - 1),
+                    )
+                nc.scalar.activation(own_sb[:, j_cols], own_ps[:], IDENTITY, bias=bias_col[:, b : b + 1])
+
+                nb_ps = psum_nb.tile([P, CHUNK], F32, name="nb_ps")
+                for g in range(GRAPHS):
+                    u_of_graph = u_bf[g // PAIR][:, g % PAIR]
+                    n_cols = slice(g * P, (g + 1) * P)
+                    nc.tensor.matmul(nb_ps[:, n_cols], lhsT=u_of_graph[:, 0], rhs=lap[:], start=True, stop=False)
+                    nc.tensor.matmul(nb_ps[:, n_cols], lhsT=u_of_graph[:, 1], rhs=cheb2[:], start=False, stop=True)
+                nc.scalar.copy(nb_sb[:, j_cols], nb_ps[:])
+
+            nc.vector.tensor_tensor(windows[b][:].indirect(offsets[:]), own_sb[:], nb_sb[:], ADD)
+            nc.sync.dma_start(out[b * P : (b + 1) * P, :], windows[b][:])

@@ -39,22 +39,27 @@ def tile_reschebgc_b_kernel(tc, x, adj, w, bias, base, offs, out):
         psum_nb = ctx.enter_context(tc.psum_pool(name="psum_nb", bufs=2))
 
         adj_sb = held.tile([P, P], F32, name="adj_sb")
-        nc.sync.dma_start(adj_sb[:], adj)
-        w_sb = held.tile([P, ORDERS, CB, CO], BF16, name="w_sb")
-        w_view = w.rearrange("k (cb c) d -> k c cb d", c=P)
+        nc.scalar.dma_start(adj_sb[:], adj)
+        bias_rows = held.tile([DB, P], F32, name="bias_rows")
+        nc.scalar.dma_start(bias_rows[:], bias.rearrange("(b d) o -> b (d o)", d=P))
+        w_sb = [held.tile([P, ORDERS, CB, P], BF16, name=f"w_sb{b}") for b in range(DB)]
+        w_view = w.rearrange("k (cb c) d -> c (k cb) d", c=P)
         x_sb = [held.tile([P, CB, CHUNK], BF16, name=f"x_sb{q}") for q in range(NQ)]
         x_view = x.rearrange("(cb c) j -> c cb j", c=P)
-        nc.sync.dma_start(w_sb[:, 1], w_view[1])
-        nc.sync.dma_start(w_sb[:, 2], w_view[2])
-        nc.sync.dma_start(x_sb[0][:], x_view[:, :, 0:CHUNK])
-        nc.sync.dma_start(w_sb[:, 0], w_view[0])
-        for q in range(1, NQ):
-            nc.sync.dma_start(x_sb[q][:], x_view[:, :, q * CHUNK : (q + 1) * CHUNK])
-        bias_rows = held.tile([DB, P], F32, name="bias_rows")
-        nc.sync.dma_start(bias_rows[:], bias.rearrange("(b d) o -> b (d o)", d=P))
         offsets = held.tile([P, N // 16], U16, name="offsets")
-        nc.sync.dma_start(offsets[:], offs)
         windows = [held.tile([P, S], F32, name=f"window{b}") for b in range(DB)]
+
+        def load_weights(b):
+            nc.sync.dma_start(
+                w_sb[b][:].rearrange("c k cb d -> c (k cb) d"), w_view[:, :, b * P : (b + 1) * P]
+            )
+
+        load_weights(0)
+        for q in range(NQ):
+            nc.sync.dma_start(x_sb[q][:], x_view[:, :, q * CHUNK : (q + 1) * CHUNK])
+        for b in range(1, DB):
+            load_weights(b)
+        nc.sync.dma_start(offsets[:], offs)
         for b in range(DB):
             nc.sync.dma_start(windows[b][:], base[b * P : (b + 1) * P, :])
 
@@ -87,7 +92,6 @@ def tile_reschebgc_b_kernel(tc, x, adj, w, bias, base, offs, out):
         nc.vector.tensor_copy(bias_col[:], bias_ps[:, 0:DB])
 
         for b in range(DB):
-            d_cols = slice(b * P, (b + 1) * P)
             own_sb = staged.tile([P, N], F32, name="own_sb")
             nb_sb = staged.tile([P, N], F32, name="nb_sb")
             for q in range(NQ):
@@ -101,7 +105,7 @@ def tile_reschebgc_b_kernel(tc, x, adj, w, bias, base, offs, out):
                             nc.tensor.matmul(
                                 u_ps[:, i],
                                 lhsT=x_sb[q][:, cb, g * P : (g + 1) * P],
-                                rhs=w_sb[:, 1:3, cb, d_cols],
+                                rhs=w_sb[b][:, 1:3, cb, :],
                                 start=(cb == 0),
                                 stop=(cb == CB - 1),
                             )
@@ -112,7 +116,7 @@ def tile_reschebgc_b_kernel(tc, x, adj, w, bias, base, offs, out):
                 for cb in range(CB):
                     nc.tensor.matmul(
                         own_ps[:],
-                        lhsT=w_sb[:, 0, cb, d_cols],
+                        lhsT=w_sb[b][:, 0, cb, :],
                         rhs=x_sb[q][:, cb, :],
                         start=(cb == 0),
                         stop=(cb == CB - 1),

@@ -23,6 +23,7 @@ CHUNK = 512
 NQ = N // CHUNK
 GRAPHS = CHUNK // P
 PAIR = 2
+WARM_MATMULS = 12
 
 FLOPS = 2 * ORDERS * CI * CO * N + 2 * 2 * P * CO * N + 2 * P * P * P
 
@@ -37,6 +38,12 @@ def tile_reschebgc_b_kernel(tc, x, adj, w, bias, base, offs, out):
         psum_u = ctx.enter_context(tc.psum_pool(name="psum_u", bufs=3))
         psum_own = ctx.enter_context(tc.psum_pool(name="psum_own", bufs=2))
         psum_nb = ctx.enter_context(tc.psum_pool(name="psum_nb", bufs=2))
+
+        zeros = held.tile([P, CHUNK], BF16, name="zeros")
+        nc.vector.memset(zeros[:], 0.0)
+        warm_ps = psum_setup.tile([P, CHUNK], F32, name="setup_ps")
+        for repeat in range(WARM_MATMULS):
+            nc.tensor.matmul(warm_ps[:], lhsT=zeros[:, 0:P], rhs=zeros[:], start=True, stop=True)
 
         adj_sb = held.tile([P, P], F32, name="adj_sb")
         nc.scalar.dma_start(adj_sb[:], adj)

@@ -23,7 +23,7 @@ CHUNK = 512
 NQ = N // CHUNK
 GRAPHS = CHUNK // P
 PAIR = 2
-WARM_MATMULS = 12
+WARM_MATMULS = 8
 
 FLOPS = 2 * ORDERS * CI * CO * N + 2 * 2 * P * CO * N + 2 * P * P * P
 
@@ -50,20 +50,23 @@ def tile_reschebgc_b_kernel(tc, x, adj, w, bias, base, offs, out):
         bias_rows = held.tile([DB, P], F32, name="bias_rows")
         nc.scalar.dma_start(bias_rows[:], bias.rearrange("(b d) o -> b (d o)", d=P))
         w_sb = [held.tile([P, ORDERS, CB, P], BF16, name=f"w_sb{b}") for b in range(DB)]
-        w_view = w.rearrange("k (cb c) d -> c (k cb) d", c=P)
+        w_view = w.rearrange("k (cb c) d -> k c cb d", c=P)
         x_sb = [held.tile([P, CB, CHUNK], BF16, name=f"x_sb{q}") for q in range(NQ)]
         x_view = x.rearrange("(cb c) j -> c cb j", c=P)
         offsets = held.tile([P, N // 16], U16, name="offsets")
         windows = [held.tile([P, S], F32, name=f"window{b}") for b in range(DB)]
 
-        def load_weights(b):
-            nc.sync.dma_start(
-                w_sb[b][:].rearrange("c k cb d -> c (k cb) d"), w_view[:, :, b * P : (b + 1) * P]
-            )
-
-        load_weights(0)
-        for q in range(NQ):
+        def load_x(q):
             nc.sync.dma_start(x_sb[q][:], x_view[:, :, q * CHUNK : (q + 1) * CHUNK])
+
+        def load_weights(b):
+            for k in range(ORDERS):
+                nc.sync.dma_start(w_sb[b][:, k], w_view[k][:, :, b * P : (b + 1) * P])
+
+        load_x(0)
+        load_weights(0)
+        for q in range(1, NQ):
+            load_x(q)
         for b in range(1, DB):
             load_weights(b)
         nc.sync.dma_start(offsets[:], offs)

@@ -23,7 +23,7 @@ CHUNK = 512
 NQ = N // CHUNK
 GRAPHS = CHUNK // P
 PAIR = 2
-WARM_MATMULS = 8
+WARM_MATMULS = 5
 
 FLOPS = 2 * ORDERS * CI * CO * N + 2 * 2 * P * CO * N + 2 * P * P * P
 
@@ -59,16 +59,19 @@ def tile_reschebgc_b_kernel(tc, x, adj, w, bias, base, offs, out):
         def load_x(q):
             nc.sync.dma_start(x_sb[q][:], x_view[:, :, q * CHUNK : (q + 1) * CHUNK])
 
-        def load_weights(b):
-            for k in range(ORDERS):
-                nc.sync.dma_start(w_sb[b][:, k], w_view[k][:, :, b * P : (b + 1) * P])
+        def load_weights(b, k):
+            nc.sync.dma_start(w_sb[b][:, k], w_view[k][:, :, b * P : (b + 1) * P])
 
-        load_x(0)
-        load_weights(0)
+        load_weights(0, 1)
+        load_weights(0, 2)
+        for g in range(GRAPHS):
+            nc.sync.dma_start(x_sb[0][:, :, g * P : (g + 1) * P], x_view[:, :, g * P : (g + 1) * P])
+        load_weights(0, 0)
         for q in range(1, NQ):
             load_x(q)
         for b in range(1, DB):
-            load_weights(b)
+            for k in range(ORDERS):
+                load_weights(b, k)
         nc.sync.dma_start(offsets[:], offs)
         for b in range(DB):
             nc.sync.dma_start(windows[b][:], base[b * P : (b + 1) * P, :])

@@ -47,8 +47,8 @@ def tile_reschebgc_b_kernel(tc, x, adj, w, bias, base, offs, out):
 
         adj_sb = held.tile([P, P], F32, name="adj_sb")
         nc.scalar.dma_start(adj_sb[:], adj)
-        bias_rows = held.tile([DB, P], F32, name="bias_rows")
-        nc.scalar.dma_start(bias_rows[:], bias.rearrange("(b d) o -> b (d o)", d=P))
+        bias_col = held.tile([P, DB], F32, name="bias_col")
+        nc.scalar.dma_start(bias_col[:], bias.rearrange("(b d) o -> d (b o)", d=P))
         w_sb = [held.tile([P, ORDERS, CB, P], BF16, name=f"w_sb{b}") for b in range(DB)]
         w_view = w.rearrange("k (cb c) d -> k c cb d", c=P)
         x_sb = [held.tile([P, CB, CHUNK], BF16, name=f"x_sb{q}") for q in range(NQ)]
@@ -78,31 +78,32 @@ def tile_reschebgc_b_kernel(tc, x, adj, w, bias, base, offs, out):
 
         ident = held.tile([P, P], F32, name="ident")
         make_identity(nc, ident[:])
+        ones = held.tile([P, P], BF16, name="ones")
+        nc.vector.memset(ones[:], 1.0)
+        adj_bf = held.tile([P, P], BF16, name="adj_bf")
+        nc.vector.tensor_copy(adj_bf[:], adj_sb[:])
+        deg_row_ps = psum_setup.tile([P, P], F32, name="setup_ps")
+        nc.tensor.matmul(deg_row_ps[:], lhsT=ones[:], rhs=adj_bf[:], start=True, stop=True)
         deg = held.tile([P, 1], F32, name="deg")
         nc.vector.reduce_sum(deg[:], adj_sb[:], axis=mybir.AxisListType.X)
         root = held.tile([P, 1], F32, name="root")
         nc.scalar.sqrt(root[:], deg[:])
+        root_row = held.tile([P, P], F32, name="root_row")
+        nc.scalar.sqrt(root_row[:], deg_row_ps[:])
         r = held.tile([P, 1], F32, name="r")
         nc.vector.reciprocal(r[:], root[:])
         minus_r = held.tile([P, 1], F32, name="minus_r")
         nc.vector.tensor_scalar_mul(minus_r[:], r[:], -1.0)
-        diag_r = held.tile([P, P], F32, name="diag_r")
-        nc.vector.tensor_scalar_mul(diag_r[:], ident[:], r[:])
-        cols_ps = psum_setup.tile([P, P], F32, name="setup_ps")
-        nc.tensor.matmul(cols_ps[:], lhsT=adj_sb[:], rhs=diag_r[:], start=True, stop=True)
+        r_row = held.tile([P, P], F32, name="r_row")
+        nc.vector.reciprocal(r_row[:], root_row[:])
+        scaled = held.tile([P, P], F32, name="scaled")
+        nc.vector.scalar_tensor_tensor(scaled[:], adj_sb[:], minus_r[:], r_row[:], op0=MULT, op1=MULT)
         lap = held.tile([P, P], BF16, name="lap")
-        nc.vector.scalar_tensor_tensor(lap[:], cols_ps[:], minus_r[:], ident[:], op0=MULT, op1=ADD)
+        nc.vector.tensor_tensor(lap[:], scaled[:], ident[:], ADD)
         square_ps = psum_setup.tile([P, P], F32, name="setup_ps")
         nc.tensor.matmul(square_ps[:], lhsT=lap[:], rhs=lap[:], start=True, stop=True)
         cheb2 = held.tile([P, P], BF16, name="cheb2")
         nc.vector.scalar_tensor_tensor(cheb2[:], square_ps[:], 2.0, ident[:], op0=MULT, op1=SUBTRACT)
-
-        bias_ps = psum_setup.tile([P, P], F32, name="setup_ps")
-        nc.tensor.matmul(
-            bias_ps[:, 0:DB], lhsT=bias_rows[:], rhs=ident[0:DB, 0:DB], start=True, stop=True
-        )
-        bias_col = held.tile([P, DB], F32, name="bias_col")
-        nc.vector.tensor_copy(bias_col[:], bias_ps[:, 0:DB])
 
         for b in range(DB):
             own_sb = staged.tile([P, N], F32, name="own_sb")

@@ -137,13 +137,18 @@ def tile_reschebgc_b_kernel(tc, x, adj, w, bias, base, offs, out):
                     )
                 nc.scalar.activation(own_sb[:, j_cols], own_ps[:], IDENTITY, bias=bias_col[:, b : b + 1])
 
-                nb_ps = psum_nb.tile([P, CHUNK], F32, name="nb_ps")
-                for g in range(GRAPHS):
-                    u_of_graph = u_bf[g // PAIR][:, g % PAIR]
-                    n_cols = slice(g * P, (g + 1) * P)
-                    nc.tensor.matmul(nb_ps[:, n_cols], lhsT=u_of_graph[:, 0], rhs=lap[:], start=True, stop=False)
-                    nc.tensor.matmul(nb_ps[:, n_cols], lhsT=u_of_graph[:, 1], rhs=cheb2[:], start=False, stop=True)
-                nc.scalar.copy(nb_sb[:, j_cols], nb_ps[:])
+                for pair in range(GRAPHS // PAIR):
+                    nb_ps = psum_nb.tile([P, PAIR * P], F32, name="nb_ps")
+                    for i in range(PAIR):
+                        u_of_graph = u_bf[pair][:, i]
+                        n_cols = slice(i * P, (i + 1) * P)
+                        nc.tensor.matmul(nb_ps[:, n_cols], lhsT=u_of_graph[:, 0], rhs=lap[:], start=True, stop=False)
+                        nc.tensor.matmul(nb_ps[:, n_cols], lhsT=u_of_graph[:, 1], rhs=cheb2[:], start=False, stop=True)
+                    pair_cols = slice(q * CHUNK + pair * PAIR * P, q * CHUNK + (pair + 1) * PAIR * P)
+                    if q == NQ - 1 and pair == GRAPHS // PAIR - 1:
+                        nc.vector.tensor_copy(nb_sb[:, pair_cols], nb_ps[:])
+                    else:
+                        nc.scalar.copy(nb_sb[:, pair_cols], nb_ps[:])
 
             nc.vector.tensor_tensor(windows[b][:].indirect(offsets[:]), own_sb[:], nb_sb[:], ADD)
             nc.sync.dma_start(out[b * P : (b + 1) * P, :], windows[b][:])

@@ -49,7 +49,7 @@ def tile_reschebgc_b_kernel(tc, x, adj, w, bias, base, offs, out):
         nc.scalar.dma_start(adj_sb[:], adj)
         bias_col = held.tile([P, DB], F32, name="bias_col")
         nc.scalar.dma_start(bias_col[:], bias.rearrange("(b d) o -> d (b o)", d=P))
-        w_sb = [held.tile([P, ORDERS, CB, P], BF16, name=f"w_sb{b}") for b in range(DB)]
+        w_sb = [held.tile([P, CB, ORDERS, P], BF16, name=f"w_sb{b}") for b in range(DB)]
         w_view = w.rearrange("k (cb c) d -> k c cb d", c=P)
         x_sb = [held.tile([P, CB, CHUNK], BF16, name=f"x_sb{q}") for q in range(NQ)]
         x_view = x.rearrange("(cb c) j -> c cb j", c=P)
@@ -60,7 +60,7 @@ def tile_reschebgc_b_kernel(tc, x, adj, w, bias, base, offs, out):
             nc.sync.dma_start(x_sb[q][:], x_view[:, :, q * CHUNK : (q + 1) * CHUNK])
 
         def load_weights(b, k):
-            nc.sync.dma_start(w_sb[b][:, k], w_view[k][:, :, b * P : (b + 1) * P])
+            nc.sync.dma_start(w_sb[b][:, :, k, :], w_view[k][:, :, b * P : (b + 1) * P])
 
         load_weights(0, 1)
         load_weights(0, 2)
@@ -119,7 +119,7 @@ def tile_reschebgc_b_kernel(tc, x, adj, w, bias, base, offs, out):
                             nc.tensor.matmul(
                                 u_ps[:, i],
                                 lhsT=x_sb[q][:, cb, g * P : (g + 1) * P],
-                                rhs=w_sb[b][:, 1:3, cb, :],
+                                rhs=w_sb[b][:, cb, 1:3, :],
                                 start=(cb == 0),
                                 stop=(cb == CB - 1),
                             )
@@ -130,7 +130,7 @@ def tile_reschebgc_b_kernel(tc, x, adj, w, bias, base, offs, out):
                 for cb in range(CB):
                     nc.tensor.matmul(
                         own_ps[:],
-                        lhsT=w_sb[b][:, 0, cb, :],
+                        lhsT=w_sb[b][:, cb, 0, :],
                         rhs=x_sb[q][:, cb, :],
                         start=(cb == 0),
                         stop=(cb == CB - 1),

@@ -23,7 +23,7 @@ CHUNK = 512
 NQ = N // CHUNK
 GRAPHS = CHUNK // P
 PAIR = 2
-WARM_MATMULS = 5
+WARM_MATMULS = 4
 
 FLOPS = 2 * ORDERS * CI * CO * N + 2 * 2 * P * CO * N + 2 * P * P * P
 
@@ -34,44 +34,45 @@ def tile_reschebgc_b_kernel(tc, x, adj, w, bias, base, offs, out):
         held = ctx.enter_context(tc.tile_pool(name="held", bufs=1))
         mixed = ctx.enter_context(tc.tile_pool(name="mixed", bufs=4))
         staged = ctx.enter_context(tc.tile_pool(name="staged", bufs=2))
-        psum_setup = ctx.enter_context(tc.psum_pool(name="psum_setup", bufs=1))
-        psum_u = ctx.enter_context(tc.psum_pool(name="psum_u", bufs=3))
+        psum_u = ctx.enter_context(tc.psum_pool(name="psum_u", bufs=4))
         psum_own = ctx.enter_context(tc.psum_pool(name="psum_own", bufs=2))
         psum_nb = ctx.enter_context(tc.psum_pool(name="psum_nb", bufs=2))
 
         zeros = held.tile([P, CHUNK], BF16, name="zeros")
         nc.vector.memset(zeros[:], 0.0)
-        warm_ps = psum_setup.tile([P, CHUNK], F32, name="setup_ps")
+        warm_ps = psum_nb.tile([P, CHUNK], F32, name="nb_ps")
         for repeat in range(WARM_MATMULS):
             nc.tensor.matmul(warm_ps[:], lhsT=zeros[:, 0:P], rhs=zeros[:], start=True, stop=True)
 
         adj_sb = held.tile([P, P], F32, name="adj_sb")
         nc.scalar.dma_start(adj_sb[:], adj)
         bias_col = held.tile([P, DB], F32, name="bias_col")
-        nc.scalar.dma_start(bias_col[:], bias.rearrange("(b d) o -> d (b o)", d=P))
-        w_sb = [held.tile([P, CB, ORDERS, P], BF16, name=f"w_sb{b}") for b in range(DB)]
-        w_view = w.rearrange("k (cb c) d -> k c cb d", c=P)
+        w_sb = [held.tile([P, CB, ORDERS, 2 * P], BF16, name=f"w_sb{h}") for h in range(DB // 2)]
+        w_view = w.rearrange("k (cb c) d -> c cb k d", c=P)
         x_sb = [held.tile([P, CB, CHUNK], BF16, name=f"x_sb{q}") for q in range(NQ)]
         x_view = x.rearrange("(cb c) j -> c cb j", c=P)
         offsets = held.tile([P, N // 16], U16, name="offsets")
         windows = [held.tile([P, S], F32, name=f"window{b}") for b in range(DB)]
 
-        def load_x(q):
-            nc.sync.dma_start(x_sb[q][:], x_view[:, :, q * CHUNK : (q + 1) * CHUNK])
+        def load_x(q, cbs):
+            nc.sync.dma_start(x_sb[q][:, cbs, :], x_view[:, cbs, q * CHUNK : (q + 1) * CHUNK])
 
-        def load_weights(b, k):
-            nc.sync.dma_start(w_sb[b][:, :, k, :], w_view[k][:, :, b * P : (b + 1) * P])
+        def load_w12(h, cb):
+            nc.sync.dma_start(w_sb[h][:, cb, 1:3, :], w_view[:, cb, 1:3, h * 2 * P : (h + 1) * 2 * P])
 
-        load_weights(0, 1)
-        load_weights(0, 2)
-        for g in range(GRAPHS):
-            nc.sync.dma_start(x_sb[0][:, :, g * P : (g + 1) * P], x_view[:, :, g * P : (g + 1) * P])
-        load_weights(0, 0)
+        def load_w0(h):
+            nc.sync.dma_start(w_sb[h][:, :, 0, :], w_view[:, :, 0, h * 2 * P : (h + 1) * 2 * P])
+
+        for cb in range(CB):
+            load_x(0, slice(cb, cb + 1))
+            load_w12(0, cb)
+        load_w0(0)
+        nc.sync.dma_start(bias_col[:], bias.rearrange("(b d) o -> d (b o)", d=P))
         for q in range(1, NQ):
-            load_x(q)
-        for b in range(1, DB):
-            for k in range(ORDERS):
-                load_weights(b, k)
+            load_x(q, slice(0, CB))
+        for cb in range(CB):
+            load_w12(1, cb)
+        load_w0(1)
         nc.sync.dma_start(offsets[:], offs)
         for b in range(DB):
             nc.sync.dma_start(windows[b][:], base[b * P : (b + 1) * P, :])
@@ -82,7 +83,7 @@ def tile_reschebgc_b_kernel(tc, x, adj, w, bias, base, offs, out):
         nc.vector.memset(ones[:], 1.0)
         adj_bf = held.tile([P, P], BF16, name="adj_bf")
         nc.vector.tensor_copy(adj_bf[:], adj_sb[:])
-        deg_row_ps = psum_setup.tile([P, P], F32, name="setup_ps")
+        deg_row_ps = psum_nb.tile([P, P], F32, name="nb_ps")
         nc.tensor.matmul(deg_row_ps[:], lhsT=ones[:], rhs=adj_bf[:], start=True, stop=True)
         deg = held.tile([P, 1], F32, name="deg")
         nc.vector.reduce_sum(deg[:], adj_sb[:], axis=mybir.AxisListType.X)
@@ -100,37 +101,67 @@ def tile_reschebgc_b_kernel(tc, x, adj, w, bias, base, offs, out):
         nc.vector.scalar_tensor_tensor(scaled[:], adj_sb[:], minus_r[:], r_row[:], op0=MULT, op1=MULT)
         lap = held.tile([P, P], BF16, name="lap")
         nc.vector.tensor_tensor(lap[:], scaled[:], ident[:], ADD)
-        square_ps = psum_setup.tile([P, P], F32, name="setup_ps")
+        square_ps = psum_nb.tile([P, P], F32, name="nb_ps")
         nc.tensor.matmul(square_ps[:], lhsT=lap[:], rhs=lap[:], start=True, stop=True)
         cheb2 = held.tile([P, P], BF16, name="cheb2")
         nc.vector.scalar_tensor_tensor(cheb2[:], square_ps[:], 2.0, ident[:], op0=MULT, op1=SUBTRACT)
 
+        def shared_u():
+            u_ps = [psum_u.tile([P, 2, 2 * P], F32, name="u_ps") for g in range(GRAPHS)]
+            for cb in range(CB):
+                for g in range(GRAPHS):
+                    nc.tensor.matmul(
+                        u_ps[g][:],
+                        lhsT=x_sb[0][:, cb, g * P : (g + 1) * P],
+                        rhs=w_sb[0][:, cb, 1:3, :],
+                        start=(cb == 0),
+                        stop=(cb == CB - 1),
+                    )
+            u_bf = [mixed.tile([P, 2, 2 * P], BF16, name="u_shared") for g in range(GRAPHS)]
+            for g in range(GRAPHS):
+                if g % 2 == 1:
+                    nc.vector.tensor_copy(u_bf[g][:], u_ps[g][:])
+                else:
+                    nc.scalar.copy(u_bf[g][:], u_ps[g][:])
+            return u_bf
+
+        def own_u(b, q):
+            d_cols = slice(b % 2 * P, (b % 2 + 1) * P)
+            u_graphs = []
+            for pair in range(GRAPHS // PAIR):
+                u_ps = psum_u.tile([P, PAIR, 2, P], F32, name="u_ps")
+                for i in range(PAIR):
+                    g = pair * PAIR + i
+                    for cb in range(CB):
+                        nc.tensor.matmul(
+                            u_ps[:, i],
+                            lhsT=x_sb[q][:, cb, g * P : (g + 1) * P],
+                            rhs=w_sb[b // 2][:, cb, 1:3, d_cols],
+                            start=(cb == 0),
+                            stop=(cb == CB - 1),
+                        )
+                u_bf = mixed.tile([P, PAIR, 2, P], BF16, name="u_bf")
+                nc.scalar.copy(u_bf[:], u_ps[:])
+                u_graphs += [u_bf[:, i] for i in range(PAIR)]
+            return u_graphs
+
+        shared = shared_u()
         for b in range(DB):
             own_sb = staged.tile([P, N], F32, name="own_sb")
             nb_sb = staged.tile([P, N], F32, name="nb_sb")
+            d_cols = slice(b % 2 * P, (b % 2 + 1) * P)
             for q in range(NQ):
                 j_cols = slice(q * CHUNK, (q + 1) * CHUNK)
-                u_bf = []
-                for pair in range(GRAPHS // PAIR):
-                    u_ps = psum_u.tile([P, PAIR, 2, P], F32, name="u_ps")
-                    for i in range(PAIR):
-                        g = pair * PAIR + i
-                        for cb in range(CB):
-                            nc.tensor.matmul(
-                                u_ps[:, i],
-                                lhsT=x_sb[q][:, cb, g * P : (g + 1) * P],
-                                rhs=w_sb[b][:, cb, 1:3, :],
-                                start=(cb == 0),
-                                stop=(cb == CB - 1),
-                            )
-                    u_bf.append(mixed.tile([P, PAIR, 2, P], BF16, name="u_bf"))
-                    nc.scalar.copy(u_bf[pair][:], u_ps[:])
+                if q == 0 and b < 2:
+                    u_graphs = [u_bf[:, :, d_cols] for u_bf in shared]
+                else:
+                    u_graphs = own_u(b, q)
 
                 own_ps = psum_own.tile([P, CHUNK], F32, name="own_ps")
                 for cb in range(CB):
                     nc.tensor.matmul(
                         own_ps[:],
-                        lhsT=w_sb[b][:, cb, 0, :],
+                        lhsT=w_sb[b // 2][:, cb, 0, d_cols],
                         rhs=x_sb[q][:, cb, :],
                         start=(cb == 0),
                         stop=(cb == CB - 1),
@@ -140,7 +171,7 @@ def tile_reschebgc_b_kernel(tc, x, adj, w, bias, base, offs, out):
                 for pair in range(GRAPHS // PAIR):
                     nb_ps = psum_nb.tile([P, PAIR * P], F32, name="nb_ps")
                     for i in range(PAIR):
-                        u_of_graph = u_bf[pair][:, i]
+                        u_of_graph = u_graphs[pair * PAIR + i]
                         n_cols = slice(i * P, (i + 1) * P)
                         nc.tensor.matmul(nb_ps[:, n_cols], lhsT=u_of_graph[:, 0], rhs=lap[:], start=True, stop=False)
                         nc.tensor.matmul(nb_ps[:, n_cols], lhsT=u_of_graph[:, 1], rhs=cheb2[:], start=False, stop=True)

@@ -23,7 +23,7 @@ CHUNK = 512
 NQ = N // CHUNK
 GRAPHS = CHUNK // P
 PAIR = 2
-WARM_MATMULS = 4
+WARM_MATMULS = 3
 
 FLOPS = 2 * ORDERS * CI * CO * N + 2 * 2 * P * CO * N + 2 * P * P * P
 

@@ -23,7 +23,7 @@ CHUNK = 512
 NQ = N // CHUNK
 GRAPHS = CHUNK // P
 PAIR = 2
-WARM_MATMULS = 3
+WARM_MATMULS = 14
 
 FLOPS = 2 * ORDERS * CI * CO * N + 2 * 2 * P * CO * N + 2 * P * P * P
 
@@ -38,14 +38,13 @@ def tile_reschebgc_b_kernel(tc, x, adj, w, bias, base, offs, out):
         psum_own = ctx.enter_context(tc.psum_pool(name="psum_own", bufs=2))
         psum_nb = ctx.enter_context(tc.psum_pool(name="psum_nb", bufs=2))
 
-        zeros = held.tile([P, CHUNK], BF16, name="zeros")
-        nc.vector.memset(zeros[:], 0.0)
-        warm_ps = psum_nb.tile([P, CHUNK], F32, name="nb_ps")
+        zeros = held.tile([P, P], BF16, name="zeros")
+        nc.gpsimd.memset(zeros[:], 0.0)
+        warm_ps = psum_nb.tile([P, P], F32, name="nb_ps")
         for repeat in range(WARM_MATMULS):
-            nc.tensor.matmul(warm_ps[:], lhsT=zeros[:, 0:P], rhs=zeros[:], start=True, stop=True)
+            nc.tensor.matmul(warm_ps[:], lhsT=zeros[:], rhs=zeros[:], start=True, stop=True)
 
         adj_sb = held.tile([P, P], F32, name="adj_sb")
-        nc.scalar.dma_start(adj_sb[:], adj)
         bias_col = held.tile([P, DB], F32, name="bias_col")
         w_sb = [held.tile([P, CB, ORDERS, 2 * P], BF16, name=f"w_sb{h}") for h in range(DB // 2)]
         w_view = w.rearrange("k (cb c) d -> c cb k d", c=P)
@@ -66,6 +65,8 @@ def tile_reschebgc_b_kernel(tc, x, adj, w, bias, base, offs, out):
         for cb in range(CB):
             load_x(0, slice(cb, cb + 1))
             load_w12(0, cb)
+            if cb == 1:
+                nc.sync.dma_start(adj_sb[:], adj)
         load_w0(0)
         nc.sync.dma_start(bias_col[:], bias.rearrange("(b d) o -> d (b o)", d=P))
         for q in range(1, NQ):
@@ -166,20 +167,27 @@ def tile_reschebgc_b_kernel(tc, x, adj, w, bias, base, offs, out):
                         start=(cb == 0),
                         stop=(cb == CB - 1),
                     )
-                nc.scalar.activation(own_sb[:, j_cols], own_ps[:], IDENTITY, bias=bias_col[:, b : b + 1])
+                kernel_end = b == DB - 1 and q == NQ - 1
+                if kernel_end:
+                    nc.vector.tensor_scalar_add(own_sb[:, j_cols], own_ps[:], bias_col[:, b : b + 1])
+                else:
+                    nc.scalar.activation(own_sb[:, j_cols], own_ps[:], IDENTITY, bias=bias_col[:, b : b + 1])
 
-                for pair in range(GRAPHS // PAIR):
-                    nb_ps = psum_nb.tile([P, PAIR * P], F32, name="nb_ps")
-                    for i in range(PAIR):
-                        u_of_graph = u_graphs[pair * PAIR + i]
-                        n_cols = slice(i * P, (i + 1) * P)
-                        nc.tensor.matmul(nb_ps[:, n_cols], lhsT=u_of_graph[:, 0], rhs=lap[:], start=True, stop=False)
-                        nc.tensor.matmul(nb_ps[:, n_cols], lhsT=u_of_graph[:, 1], rhs=cheb2[:], start=False, stop=True)
-                    pair_cols = slice(q * CHUNK + pair * PAIR * P, q * CHUNK + (pair + 1) * PAIR * P)
-                    if q == NQ - 1 and pair == GRAPHS // PAIR - 1:
-                        nc.vector.tensor_copy(nb_sb[:, pair_cols], nb_ps[:])
+                graph_groups = [(0, 1), (2,), (3,)] if kernel_end else [(0, 1), (2, 3)]
+                for graphs in graph_groups:
+                    if len(graphs) == PAIR:
+                        nb_ps = psum_nb.tile([P, PAIR * P], F32, name="nb_ps")
                     else:
-                        nc.scalar.copy(nb_sb[:, pair_cols], nb_ps[:])
+                        nb_ps = psum_u.tile([P, P], F32, name="u_ps")
+                    for i, g in enumerate(graphs):
+                        n_cols = slice(i * P, (i + 1) * P)
+                        nc.tensor.matmul(nb_ps[:, n_cols], lhsT=u_graphs[g][:, 0], rhs=lap[:], start=True, stop=False)
+                        nc.tensor.matmul(nb_ps[:, n_cols], lhsT=u_graphs[g][:, 1], rhs=cheb2[:], start=False, stop=True)
+                    group_cols = slice(q * CHUNK + graphs[0] * P, q * CHUNK + (graphs[-1] + 1) * P)
+                    if kernel_end and graphs[-1] == GRAPHS - 1:
+                        nc.vector.tensor_copy(nb_sb[:, group_cols], nb_ps[:])
+                    else:
+                        nc.scalar.copy(nb_sb[:, group_cols], nb_ps[:])
 
             nc.vector.tensor_tensor(windows[b][:].indirect(offsets[:]), own_sb[:], nb_sb[:], ADD)
             nc.sync.dma_start(out[b * P : (b + 1) * P, :], windows[b][:])

@@ -22,6 +22,7 @@ DB = CO // P
 CHUNK = 512
 NQ = N // CHUNK
 GRAPHS = CHUNK // P
+SHARED_CHUNKS = {0: (0, 1), 1: (3,), 2: (), 3: ()}
 PAIR = 2
 WARM_MATMULS = 14
 
@@ -33,6 +34,7 @@ def tile_reschebgc_b_kernel(tc, x, adj, w, bias, base, offs, out):
     with ExitStack() as ctx:
         held = ctx.enter_context(tc.tile_pool(name="held", bufs=1))
         mixed = ctx.enter_context(tc.tile_pool(name="mixed", bufs=4))
+        kept = ctx.enter_context(tc.tile_pool(name="kept", bufs=3 * GRAPHS))
         staged = ctx.enter_context(tc.tile_pool(name="staged", bufs=2))
         psum_u = ctx.enter_context(tc.psum_pool(name="psum_u", bufs=4))
         psum_own = ctx.enter_context(tc.psum_pool(name="psum_own", bufs=2))
@@ -46,7 +48,7 @@ def tile_reschebgc_b_kernel(tc, x, adj, w, bias, base, offs, out):
 
         adj_sb = held.tile([P, P], F32, name="adj_sb")
         bias_col = held.tile([P, DB], F32, name="bias_col")
-        w_sb = [held.tile([P, CB, ORDERS, 2 * P], BF16, name=f"w_sb{h}") for h in range(DB // 2)]
+        w_sb = held.tile([P, CB, ORDERS, CO], BF16, name="w_sb")
         w_view = w.rearrange("k (cb c) d -> c cb k d", c=P)
         x_sb = [held.tile([P, CB, CHUNK], BF16, name=f"x_sb{q}") for q in range(NQ)]
         x_view = x.rearrange("(cb c) j -> c cb j", c=P)
@@ -56,11 +58,13 @@ def tile_reschebgc_b_kernel(tc, x, adj, w, bias, base, offs, out):
         def load_x(q, cbs):
             nc.sync.dma_start(x_sb[q][:, cbs, :], x_view[:, cbs, q * CHUNK : (q + 1) * CHUNK])
 
-        def load_w12(h, cb):
-            nc.sync.dma_start(w_sb[h][:, cb, 1:3, :], w_view[:, cb, 1:3, h * 2 * P : (h + 1) * 2 * P])
+        def load_w12(half, cb):
+            d_cols = slice(half * CO // 2, (half + 1) * CO // 2)
+            nc.sync.dma_start(w_sb[:, cb, 1:3, d_cols], w_view[:, cb, 1:3, d_cols])
 
-        def load_w0(h):
-            nc.sync.dma_start(w_sb[h][:, :, 0, :], w_view[:, :, 0, h * 2 * P : (h + 1) * 2 * P])
+        def load_w0(half):
+            d_cols = slice(half * CO // 2, (half + 1) * CO // 2)
+            nc.sync.dma_start(w_sb[:, :, 0, d_cols], w_view[:, :, 0, d_cols])
 
         for cb in range(CB):
             load_x(0, slice(cb, cb + 1))
@@ -107,27 +111,29 @@ def tile_reschebgc_b_kernel(tc, x, adj, w, bias, base, offs, out):
         cheb2 = held.tile([P, P], BF16, name="cheb2")
         nc.vector.scalar_tensor_tensor(cheb2[:], square_ps[:], 2.0, ident[:], op0=MULT, op1=SUBTRACT)
 
-        def shared_u():
+        def shared_u(b, q):
             u_ps = [psum_u.tile([P, 2, 2 * P], F32, name="u_ps") for g in range(GRAPHS)]
-            for cb in range(CB):
-                for g in range(GRAPHS):
-                    nc.tensor.matmul(
-                        u_ps[g][:],
-                        lhsT=x_sb[0][:, cb, g * P : (g + 1) * P],
-                        rhs=w_sb[0][:, cb, 1:3, :],
-                        start=(cb == 0),
-                        stop=(cb == CB - 1),
-                    )
-            u_bf = [mixed.tile([P, 2, 2 * P], BF16, name="u_shared") for g in range(GRAPHS)]
+            if b == 0 and q == 0:
+                passes = [(cb, g) for cb in range(CB) for g in range(GRAPHS)]
+            else:
+                passes = [(cb, g) for g in range(GRAPHS) for cb in range(CB)]
+            for cb, g in passes:
+                nc.tensor.matmul(
+                    u_ps[g][:],
+                    lhsT=x_sb[q][:, cb, g * P : (g + 1) * P],
+                    rhs=w_sb[:, cb, 1:3, b * P : (b + 2) * P],
+                    start=(cb == 0),
+                    stop=(cb == CB - 1),
+                )
+            u_bf = [kept.tile([P, 2, 2 * P], BF16, name="u_shared") for g in range(GRAPHS)]
             for g in range(GRAPHS):
-                if g % 2 == 1:
+                if b == 0 and g % 2 == 1:
                     nc.vector.tensor_copy(u_bf[g][:], u_ps[g][:])
                 else:
                     nc.scalar.copy(u_bf[g][:], u_ps[g][:])
-            return u_bf
+            return [[u[:, :, i * P : (i + 1) * P] for u in u_bf] for i in range(2)]
 
-        def own_u(b, q):
-            d_cols = slice(b % 2 * P, (b % 2 + 1) * P)
+        def single_u(b, q):
             u_graphs = []
             for pair in range(GRAPHS // PAIR):
                 u_ps = psum_u.tile([P, PAIR, 2, P], F32, name="u_ps")
@@ -137,37 +143,39 @@ def tile_reschebgc_b_kernel(tc, x, adj, w, bias, base, offs, out):
                         nc.tensor.matmul(
                             u_ps[:, i],
                             lhsT=x_sb[q][:, cb, g * P : (g + 1) * P],
-                            rhs=w_sb[b // 2][:, cb, 1:3, d_cols],
+                            rhs=w_sb[:, cb, 1:3, b * P : (b + 1) * P],
                             start=(cb == 0),
                             stop=(cb == CB - 1),
                         )
                 u_bf = mixed.tile([P, PAIR, 2, P], BF16, name="u_bf")
                 nc.scalar.copy(u_bf[:], u_ps[:])
                 u_graphs += [u_bf[:, i] for i in range(PAIR)]
-            return u_graphs
+            return [u_graphs]
 
-        shared = shared_u()
+        u_ready = {}
         for b in range(DB):
             own_sb = staged.tile([P, N], F32, name="own_sb")
             nb_sb = staged.tile([P, N], F32, name="nb_sb")
-            d_cols = slice(b % 2 * P, (b % 2 + 1) * P)
-            for q in range(NQ):
+            ready = [q for q in range(NQ) if (b, q) in u_ready]
+            chunks = ready + [q for q in range(NQ) if q not in ready]
+            for q in chunks:
                 j_cols = slice(q * CHUNK, (q + 1) * CHUNK)
-                if q == 0 and b < 2:
-                    u_graphs = [u_bf[:, :, d_cols] for u_bf in shared]
-                else:
-                    u_graphs = own_u(b, q)
+                if q not in ready:
+                    made = shared_u(b, q) if q in SHARED_CHUNKS[b] else single_u(b, q)
+                    for i, u_graphs in enumerate(made):
+                        u_ready[b + i, q] = u_graphs
+                u_graphs = u_ready[b, q]
 
                 own_ps = psum_own.tile([P, CHUNK], F32, name="own_ps")
                 for cb in range(CB):
                     nc.tensor.matmul(
                         own_ps[:],
-                        lhsT=w_sb[b // 2][:, cb, 0, d_cols],
+                        lhsT=w_sb[:, cb, 0, b * P : (b + 1) * P],
                         rhs=x_sb[q][:, cb, :],
                         start=(cb == 0),
                         stop=(cb == CB - 1),
                     )
-                kernel_end = b == DB - 1 and q == NQ - 1
+                kernel_end = b == DB - 1 and q == chunks[-1]
                 if kernel_end:
                     nc.vector.tensor_scalar_add(own_sb[:, j_cols], own_ps[:], bias_col[:, b : b + 1])
                 else:

@@ -24,7 +24,7 @@ NQ = N // CHUNK
 GRAPHS = CHUNK // P
 SHARED_CHUNKS = {0: (0, 1), 1: (3,), 2: (), 3: ()}
 PAIR = 2
-WARM_MATMULS = 14
+WARM_MATMULS = 10
 
 FLOPS = 2 * ORDERS * CI * CO * N + 2 * 2 * P * CO * N + 2 * P * P * P
 

@@ -55,20 +55,24 @@ def tile_reschebgc_b_kernel(tc, x, adj, w, bias, base, offs, out):
         offsets = held.tile([P, N // 16], U16, name="offsets")
         windows = [held.tile([P, S], F32, name=f"window{b}") for b in range(DB)]
 
-        def load_x(q, cbs):
-            nc.sync.dma_start(x_sb[q][:, cbs, :], x_view[:, cbs, q * CHUNK : (q + 1) * CHUNK])
+        def load_x(q, cbs, parts=1):
+            width = CHUNK // parts
+            for part in range(parts):
+                j = q * CHUNK + part * width
+                nc.sync.dma_start(x_sb[q][:, cbs, part * width : (part + 1) * width], x_view[:, cbs, j : j + width])
 
         def load_w12(half, cb):
             d_cols = slice(half * CO // 2, (half + 1) * CO // 2)
-            nc.sync.dma_start(w_sb[:, cb, 1:3, d_cols], w_view[:, cb, 1:3, d_cols])
+            queue = nc.scalar if half == 0 and cb == 0 else nc.sync
+            queue.dma_start(w_sb[:, cb, 1:3, d_cols], w_view[:, cb, 1:3, d_cols])
 
         def load_w0(half):
             d_cols = slice(half * CO // 2, (half + 1) * CO // 2)
             nc.sync.dma_start(w_sb[:, :, 0, d_cols], w_view[:, :, 0, d_cols])
 
         for cb in range(CB):
-            load_x(0, slice(cb, cb + 1))
             load_w12(0, cb)
+            load_x(0, slice(cb, cb + 1), parts=2 if cb == 0 else 1)
             if cb == 1:
                 nc.sync.dma_start(adj_sb[:], adj)
         load_w0(0)

@@ -185,10 +185,10 @@ def tile_reschebgc_b_kernel(tc, x, adj, w, bias, base, offs, out):
                 else:
                     nc.scalar.activation(own_sb[:, j_cols], own_ps[:], IDENTITY, bias=bias_col[:, b : b + 1])
 
-                graph_groups = [(0, 1), (2,), (3,)] if kernel_end else [(0, 1), (2, 3)]
+                graph_groups = [(0, 1), (2,), (3,)] if kernel_end else [(0, 1, 2, 3)]
                 for graphs in graph_groups:
-                    if len(graphs) == PAIR:
-                        nb_ps = psum_nb.tile([P, PAIR * P], F32, name="nb_ps")
+                    if len(graphs) > 1:
+                        nb_ps = psum_nb.tile([P, len(graphs) * P], F32, name="nb_ps")
                     else:
                         nb_ps = psum_u.tile([P, P], F32, name="u_ps")
                     for i, g in enumerate(graphs):

from contextlib import ExitStack

import concourse.mybir as mybir
from concourse.masks import make_identity

F32 = mybir.dt.float32
BF16 = mybir.dt.bfloat16
U16 = mybir.dt.uint16
ADD = mybir.AluOpType.add
MULT = mybir.AluOpType.mult
SUBTRACT = mybir.AluOpType.subtract
IDENTITY = mybir.ActivationFunctionType.Identity

P = 128
ORDERS = 3
CI = 512
CO = 512
N = 2048
S = 4096
CB = CI // P
DB = CO // P
CHUNK = 512
NQ = N // CHUNK
GRAPHS = CHUNK // P
SHARED_CHUNKS = {0: (0, 1), 1: (3,), 2: (), 3: ()}
PAIR = 2
WARM_MATMULS = 10

FLOPS = 2 * ORDERS * CI * CO * N + 2 * 2 * P * CO * N + 2 * P * P * P


def tile_reschebgc_b_kernel(tc, x, adj, w, bias, base, offs, out):
    nc = tc.nc
    with ExitStack() as ctx:
        held = ctx.enter_context(tc.tile_pool(name="held", bufs=1))
        mixed = ctx.enter_context(tc.tile_pool(name="mixed", bufs=4))
        kept = ctx.enter_context(tc.tile_pool(name="kept", bufs=3 * GRAPHS))
        staged = ctx.enter_context(tc.tile_pool(name="staged", bufs=2))
        psum_u = ctx.enter_context(tc.psum_pool(name="psum_u", bufs=4))
        psum_own = ctx.enter_context(tc.psum_pool(name="psum_own", bufs=2))
        psum_nb = ctx.enter_context(tc.psum_pool(name="psum_nb", bufs=2))

        zeros = held.tile([P, P], BF16, name="zeros")
        nc.gpsimd.memset(zeros[:], 0.0)
        warm_ps = psum_nb.tile([P, P], F32, name="nb_ps")
        for repeat in range(WARM_MATMULS):
            nc.tensor.matmul(warm_ps[:], lhsT=zeros[:], rhs=zeros[:], start=True, stop=True)

        adj_sb = held.tile([P, P], F32, name="adj_sb")
        bias_col = held.tile([P, DB], F32, name="bias_col")
        w_sb = held.tile([P, CB, ORDERS, CO], BF16, name="w_sb")
        w_view = w.rearrange("k (cb c) d -> c cb k d", c=P)
        x_sb = [held.tile([P, CB, CHUNK], BF16, name=f"x_sb{q}") for q in range(NQ)]
        x_view = x.rearrange("(cb c) j -> c cb j", c=P)
        offsets = held.tile([P, N // 16], U16, name="offsets")
        windows = [held.tile([P, S], F32, name=f"window{b}") for b in range(DB)]

        def load_x(q, cbs, parts=1):
            width = CHUNK // parts
            for part in range(parts):
                j = q * CHUNK + part * width
                nc.sync.dma_start(x_sb[q][:, cbs, part * width : (part + 1) * width], x_view[:, cbs, j : j + width])

        def load_w12(half, cb):
            d_cols = slice(half * CO // 2, (half + 1) * CO // 2)
            queue = nc.scalar if half == 0 and cb == 0 else nc.sync
            queue.dma_start(w_sb[:, cb, 1:3, d_cols], w_view[:, cb, 1:3, d_cols])

        def load_w0(half):
            d_cols = slice(half * CO // 2, (half + 1) * CO // 2)
            nc.sync.dma_start(w_sb[:, :, 0, d_cols], w_view[:, :, 0, d_cols])

        for cb in range(CB):
            load_w12(0, cb)
            load_x(0, slice(cb, cb + 1), parts=2 if cb == 0 else 1)
            if cb == 1:
                nc.sync.dma_start(adj_sb[:], adj)
        load_w0(0)
        nc.sync.dma_start(bias_col[:], bias.rearrange("(b d) o -> d (b o)", d=P))
        for q in range(1, NQ):
            load_x(q, slice(0, CB))
        for cb in range(CB):
            load_w12(1, cb)
        load_w0(1)
        nc.sync.dma_start(offsets[:], offs)
        for b in range(DB):
            nc.sync.dma_start(windows[b][:], base[b * P : (b + 1) * P, :])

        ident = held.tile([P, P], F32, name="ident")
        make_identity(nc, ident[:])
        ones = held.tile([P, P], BF16, name="ones")
        nc.vector.memset(ones[:], 1.0)
        adj_bf = held.tile([P, P], BF16, name="adj_bf")
        nc.vector.tensor_copy(adj_bf[:], adj_sb[:])
        deg_row_ps = psum_nb.tile([P, P], F32, name="nb_ps")
        nc.tensor.matmul(deg_row_ps[:], lhsT=ones[:], rhs=adj_bf[:], start=True, stop=True)
        deg = held.tile([P, 1], F32, name="deg")
        nc.vector.reduce_sum(deg[:], adj_sb[:], axis=mybir.AxisListType.X)
        root = held.tile([P, 1], F32, name="root")
        nc.scalar.sqrt(root[:], deg[:])
        root_row = held.tile([P, P], F32, name="root_row")
        nc.scalar.sqrt(root_row[:], deg_row_ps[:])
        r = held.tile([P, 1], F32, name="r")
        nc.vector.reciprocal(r[:], root[:])
        minus_r = held.tile([P, 1], F32, name="minus_r")
        nc.vector.tensor_scalar_mul(minus_r[:], r[:], -1.0)
        r_row = held.tile([P, P], F32, name="r_row")
        nc.vector.reciprocal(r_row[:], root_row[:])
        scaled = held.tile([P, P], F32, name="scaled")
        nc.vector.scalar_tensor_tensor(scaled[:], adj_sb[:], minus_r[:], r_row[:], op0=MULT, op1=MULT)
        lap = held.tile([P, P], BF16, name="lap")
        nc.vector.tensor_tensor(lap[:], scaled[:], ident[:], ADD)
        square_ps = psum_nb.tile([P, P], F32, name="nb_ps")
        nc.tensor.matmul(square_ps[:], lhsT=lap[:], rhs=lap[:], start=True, stop=True)
        cheb2 = held.tile([P, P], BF16, name="cheb2")
        nc.vector.scalar_tensor_tensor(cheb2[:], square_ps[:], 2.0, ident[:], op0=MULT, op1=SUBTRACT)

        def shared_u(b, q):
            u_ps = [psum_u.tile([P, 2, 2 * P], F32, name="u_ps") for g in range(GRAPHS)]
            if b == 0 and q == 0:
                passes = [(cb, g) for cb in range(CB) for g in range(GRAPHS)]
            else:
                passes = [(cb, g) for g in range(GRAPHS) for cb in range(CB)]
            for cb, g in passes:
                nc.tensor.matmul(
                    u_ps[g][:],
                    lhsT=x_sb[q][:, cb, g * P : (g + 1) * P],
                    rhs=w_sb[:, cb, 1:3, b * P : (b + 2) * P],
                    start=(cb == 0),
                    stop=(cb == CB - 1),
                )
            u_bf = [kept.tile([P, 2, 2 * P], BF16, name="u_shared") for g in range(GRAPHS)]
            for g in range(GRAPHS):
                if b == 0 and g % 2 == 1:
                    nc.vector.tensor_copy(u_bf[g][:], u_ps[g][:])
                else:
                    nc.scalar.copy(u_bf[g][:], u_ps[g][:])
            return [[u[:, :, i * P : (i + 1) * P] for u in u_bf] for i in range(2)]

        def single_u(b, q):
            u_graphs = []
            for pair in range(GRAPHS // PAIR):
                u_ps = psum_u.tile([P, PAIR, 2, P], F32, name="u_ps")
                for i in range(PAIR):
                    g = pair * PAIR + i
                    for cb in range(CB):
                        nc.tensor.matmul(
                            u_ps[:, i],
                            lhsT=x_sb[q][:, cb, g * P : (g + 1) * P],
                            rhs=w_sb[:, cb, 1:3, b * P : (b + 1) * P],
                            start=(cb == 0),
                            stop=(cb == CB - 1),
                        )
                u_bf = mixed.tile([P, PAIR, 2, P], BF16, name="u_bf")
                nc.scalar.copy(u_bf[:], u_ps[:])
                u_graphs += [u_bf[:, i] for i in range(PAIR)]
            return [u_graphs]

        u_ready = {}
        for b in range(DB):
            own_sb = staged.tile([P, N], F32, name="own_sb")
            nb_sb = staged.tile([P, N], F32, name="nb_sb")
            ready = [q for q in range(NQ) if (b, q) in u_ready]
            chunks = ready + [q for q in range(NQ) if q not in ready]
            for q in chunks:
                j_cols = slice(q * CHUNK, (q + 1) * CHUNK)
                if q not in ready:
                    made = shared_u(b, q) if q in SHARED_CHUNKS[b] else single_u(b, q)
                    for i, u_graphs in enumerate(made):
                        u_ready[b + i, q] = u_graphs
                u_graphs = u_ready[b, q]

                own_ps = psum_own.tile([P, CHUNK], F32, name="own_ps")
                for cb in range(CB):
                    nc.tensor.matmul(
                        own_ps[:],
                        lhsT=w_sb[:, cb, 0, b * P : (b + 1) * P],
                        rhs=x_sb[q][:, cb, :],
                        start=(cb == 0),
                        stop=(cb == CB - 1),
                    )
                kernel_end = b == DB - 1 and q == chunks[-1]
                if kernel_end:
                    nc.vector.tensor_scalar_add(own_sb[:, j_cols], own_ps[:], bias_col[:, b : b + 1])
                else:
                    nc.scalar.activation(own_sb[:, j_cols], own_ps[:], IDENTITY, bias=bias_col[:, b : b + 1])

                graph_groups = [(0, 1), (2,), (3,)] if kernel_end else [(0, 1, 2, 3)]
                for graphs in graph_groups:
                    if len(graphs) > 1:
                        nb_ps = psum_nb.tile([P, len(graphs) * P], F32, name="nb_ps")
                    else:
                        nb_ps = psum_u.tile([P, P], F32, name="u_ps")
                    for i, g in enumerate(graphs):
                        n_cols = slice(i * P, (i + 1) * P)
                        nc.tensor.matmul(nb_ps[:, n_cols], lhsT=u_graphs[g][:, 0], rhs=lap[:], start=True, stop=False)
                        nc.tensor.matmul(nb_ps[:, n_cols], lhsT=u_graphs[g][:, 1], rhs=cheb2[:], start=False, stop=True)
                    group_cols = slice(q * CHUNK + graphs[0] * P, q * CHUNK + (graphs[-1] + 1) * P)
                    if kernel_end and graphs[-1] == GRAPHS - 1:
                        nc.vector.tensor_copy(nb_sb[:, group_cols], nb_ps[:])
                    else:
                        nc.scalar.copy(nb_sb[:, group_cols], nb_ps[:])

            nc.vector.tensor_tensor(windows[b][:].indirect(offsets[:]), own_sb[:], nb_sb[:], ADD)
            nc.sync.dma_start(out[b * P : (b + 1) * P, :], windows[b][:])
